import numpy as np
import ml_dtypes

BF16 = ml_dtypes.bfloat16


def bf(x):
    return np.asarray(x, np.float32).astype(BF16)


def f32(x):
    return np.asarray(x, np.float32)


def f64(x):
    return np.asarray(x).astype(np.float64)


def striped(idx):
    return np.tile(idx.reshape(-1, 16).T, (8, 1))


D, S, N, H, P, LEV = 512, 512, 4096, 256, 128, 4


def setup_inputs():
    idx = np.concatenate([np.random.permutation(S)[:H] for _ in range(N // H)])
    return {"x": f32(np.random.standard_normal((D, S))), "right": f32(np.random.standard_normal((D, N))), "wl": bf(np.random.standard_normal((D, D)) / np.sqrt(D)), "bl": f32(0.1 * np.random.standard_normal((D, 1))), "wp": bf(np.random.standard_normal((D, P)) / np.sqrt(D)), "bp": f32(0.1 * np.random.standard_normal((P, 1))), "offs": striped(idx)}


def reference(x, right, wl, bl, wp, bp, offs):
    idx = offs[:16].T.reshape(-1)
    s = f64(x)[:, idx] + f64(right)
    outs = []
    for _ in range(LEV):
        h = np.maximum(f64(wl).T @ s + 2.0 * f64(bl), 0.0)
        outs.append(f64(wp).T @ h + f64(bp))
        s = h[:, 0::2] + h[:, 1::2]
    return np.concatenate(outs, axis=1)

@@ -1,0 +1,118 @@
+import concourse.mybir as mybir
+
+F32 = mybir.dt.float32
+BF16 = mybir.dt.bfloat16
+U16 = mybir.dt.uint16
+ADD = mybir.AluOpType.add
+RELU = mybir.ActivationFunctionType.Relu
+
+P = 128
+D = 512
+KB = D // P
+WORDS = 512
+N = 4096
+LABELS = 128
+LEVELS = 4
+C = 512
+HALF = C // 2
+OUT_START = {t: sum(N >> (u - 1) for u in range(1, t)) for t in range(1, LEVELS + 1)}
+OUT_COLUMNS = OUT_START[LEVELS] + (N >> (LEVELS - 1))
+
+FLOPS = 2 * D * (D + LABELS) * OUT_COLUMNS
+
+
+def tile_rnn_model_b_kernel(tc, x, right, wl, bl, wp, bp, offs, out):
+    nc = tc.nc
+    with (
+        tc.tile_pool(name="held", bufs=1) as held,
+        tc.tile_pool(name="leaves", bufs=N // C) as leaves,
+        tc.tile_pool(name="sums", bufs=4) as sums,
+        tc.tile_pool(name="nodes", bufs=2) as nodes,
+        tc.tile_pool(name="staged", bufs=3) as staged,
+        tc.psum_pool(name="layer_banks", bufs=4) as layer_banks,
+        tc.psum_pool(name="label_banks", bufs=2) as label_banks,
+    ):
+        offsets = held.tile([P, N // 16], U16, name="offsets")
+        nc.sync.dma_start(offsets[:], offs)
+
+        x_blocks = x.rearrange("(k p) s -> k p s", p=P)
+        right_blocks = right.rearrange("(k p) n -> k p n", p=P)
+        table = [held.tile([P, WORDS], F32, name=f"table{k}") for k in range(KB)]
+
+        def load_right(c):
+            right_c = leaves.tile([P, KB, C], F32, name="right_c")
+            for k in range(KB):
+                if c == 0:
+                    nc.sync.dma_start(table[k][:], x_blocks[k])
+                nc.sync.dma_start(right_c[:, k, :], right_blocks[k][:, c * C : (c + 1) * C])
+            return right_c
+
+        right_chunks = [load_right(c) for c in range(N // C)]
+
+        wl_sb = held.tile([P, KB, D], BF16, name="wl_sb")
+        nc.scalar.dma_start(wl_sb[:], wl.rearrange("(k p) m -> p k m", p=P))
+        wp_sb = held.tile([P, KB, LABELS], BF16, name="wp_sb")
+        nc.scalar.dma_start(wp_sb[:], wp.rearrange("(k p) l -> p k l", p=P))
+        bl_sb = held.tile([P, KB], F32, name="bl_sb")
+        nc.scalar.dma_start(bl_sb[:], bl.rearrange("(a p) o -> p (a o)", p=P))
+        bp_sb = held.tile([P, 1], F32, name="bp_sb")
+        nc.scalar.dma_start(bp_sb[:], bp)
+        twice_bl = held.tile([P, KB], F32, name="twice_bl")
+        nc.vector.tensor_scalar_mul(twice_bl[:], bl_sb[:], 2.0)
+
+        def leaf_sums(c):
+            s = nodes.tile([P, KB, C], BF16, name="s0")
+            piece = offsets[:, c * (C // 16) : (c + 1) * (C // 16)]
+            for k in range(KB):
+                exact = sums.tile([P, C], F32, name="exact")
+                nc.vector.tensor_tensor(
+                    exact[:], table[k][:].indirect(piece), right_chunks[c][:, k, :], ADD
+                )
+                nc.scalar.copy(s[:, k, :], exact[:])
+            return s
+
+        def layer(s, level):
+            h = nodes.tile([P, KB, C], BF16, name=f"h{level}")
+            for m in range(KB):
+                bank = layer_banks.tile([P, C], F32, name="bank")
+                for k in range(KB):
+                    nc.tensor.matmul(
+                        bank[:],
+                        wl_sb[:, k, m * P : (m + 1) * P],
+                        s[:, k, :],
+                        start=(k == 0),
+                        stop=(k == KB - 1),
+                    )
+                nc.scalar.activation(h[:, m, :], bank[:], RELU, bias=twice_bl[:, m : m + 1])
+            return h
+
+        def project(h, level, c):
+            bank = label_banks.tile([P, C], F32, name="label_bank")
+            for k in range(KB):
+                nc.tensor.matmul(
+                    bank[:], wp_sb[:, k, :], h[:, k, :], start=(k == 0), stop=(k == KB - 1)
+                )
+            labels = staged.tile([P, C], F32, name="labels")
+            nc.vector.tensor_scalar_add(labels[:], bank[:], bp_sb[:, 0:1])
+            first = OUT_START[level] + c * C
+            nc.sync.dma_start(out[:, first : first + C], labels[:])
+
+        def subtree(level, c):
+            if level == 1:
+                s = leaf_sums(c)
+            else:
+                s = nodes.tile([P, KB, C], BF16, name=f"s{level - 1}")
+                for side in range(2):
+                    child = subtree(level - 1, 2 * c + side)
+                    for k in range(KB):
+                        nc.vector.tensor_tensor(
+                            s[:, k, side * HALF : (side + 1) * HALF],
+                            child[:, k, 0:C:2],
+                            child[:, k, 1:C:2],
+                            ADD,
+                        )
+            h = layer(s, level)
+            project(h, level, c)
+            return h
+
+        subtree(LEVELS, 0)

@@ -5,6 +5,7 @@ BF16 = mybir.dt.bfloat16
 U16 = mybir.dt.uint16
 ADD = mybir.AluOpType.add
 RELU = mybir.ActivationFunctionType.Relu
+IDENTITY = mybir.ActivationFunctionType.Identity
 
 P = 128
 D = 512
@@ -17,6 +18,7 @@ C = 512
 HALF = C // 2
 OUT_START = {t: sum(N >> (u - 1) for u in range(1, t)) for t in range(1, LEVELS + 1)}
 OUT_COLUMNS = OUT_START[LEVELS] + (N >> (LEVELS - 1))
+AHEAD = 2
 
 FLOPS = 2 * D * (D + LABELS) * OUT_COLUMNS
 
@@ -27,32 +29,35 @@ def tile_rnn_model_b_kernel(tc, x, right, wl, bl, wp, bp, offs, out):
         tc.tile_pool(name="held", bufs=1) as held,
         tc.tile_pool(name="leaves", bufs=N // C) as leaves,
         tc.tile_pool(name="sums", bufs=4) as sums,
-        tc.tile_pool(name="nodes", bufs=2) as nodes,
+        tc.tile_pool(name="inputs", bufs=AHEAD + 2) as inputs,
+        tc.tile_pool(name="hidden", bufs=4) as hidden,
         tc.tile_pool(name="staged", bufs=3) as staged,
-        tc.psum_pool(name="layer_banks", bufs=4) as layer_banks,
-        tc.psum_pool(name="label_banks", bufs=2) as label_banks,
+        tc.psum_pool(name="layer_banks", bufs=5) as layer_banks,
+        tc.psum_pool(name="label_banks", bufs=3) as label_banks,
     ):
         offsets = held.tile([P, N // 16], U16, name="offsets")
         nc.sync.dma_start(offsets[:], offs)
 
+        table = [held.tile([P, WORDS], F32, name=f"table{k}") for k in range(KB)]
+        wl_sb = held.tile([P, KB, D], BF16, name="wl_sb")
+        wp_sb = held.tile([P, KB, LABELS], BF16, name="wp_sb")
         x_blocks = x.rearrange("(k p) s -> k p s", p=P)
         right_blocks = right.rearrange("(k p) n -> k p n", p=P)
-        table = [held.tile([P, WORDS], F32, name=f"table{k}") for k in range(KB)]
+        wl_blocks = wl.rearrange("(k p) m -> k p m", p=P)
 
-        def load_right(c):
+        right_chunks = []
+        for c in range(N // C):
             right_c = leaves.tile([P, KB, C], F32, name="right_c")
             for k in range(KB):
                 if c == 0:
                     nc.sync.dma_start(table[k][:], x_blocks[k])
                 nc.sync.dma_start(right_c[:, k, :], right_blocks[k][:, c * C : (c + 1) * C])
-            return right_c
+                if c == 0:
+                    nc.sync.dma_start(wl_sb[:, k, :], wl_blocks[k])
+            if c == 0:
+                nc.sync.dma_start(wp_sb[:], wp.rearrange("(k p) l -> p k l", p=P))
+            right_chunks.append(right_c)
 
-        right_chunks = [load_right(c) for c in range(N // C)]
-
-        wl_sb = held.tile([P, KB, D], BF16, name="wl_sb")
-        nc.scalar.dma_start(wl_sb[:], wl.rearrange("(k p) m -> p k m", p=P))
-        wp_sb = held.tile([P, KB, LABELS], BF16, name="wp_sb")
-        nc.scalar.dma_start(wp_sb[:], wp.rearrange("(k p) l -> p k l", p=P))
         bl_sb = held.tile([P, KB], F32, name="bl_sb")
         nc.scalar.dma_start(bl_sb[:], bl.rearrange("(a p) o -> p (a o)", p=P))
         bp_sb = held.tile([P, 1], F32, name="bp_sb")
@@ -61,7 +66,7 @@ def tile_rnn_model_b_kernel(tc, x, right, wl, bl, wp, bp, offs, out):
         nc.vector.tensor_scalar_mul(twice_bl[:], bl_sb[:], 2.0)
 
         def leaf_sums(c):
-            s = nodes.tile([P, KB, C], BF16, name="s0")
+            s = inputs.tile([P, KB, C], BF16, name="s0")
             piece = offsets[:, c * (C // 16) : (c + 1) * (C // 16)]
             for k in range(KB):
                 exact = sums.tile([P, C], F32, name="exact")
@@ -71,8 +76,8 @@ def tile_rnn_model_b_kernel(tc, x, right, wl, bl, wp, bp, offs, out):
                 nc.scalar.copy(s[:, k, :], exact[:])
             return s
 
-        def layer(s, level):
-            h = nodes.tile([P, KB, C], BF16, name=f"h{level}")
+        def layer(s):
+            h = hidden.tile([P, KB, C], BF16, name="h")
             for m in range(KB):
                 bank = layer_banks.tile([P, C], F32, name="bank")
                 for k in range(KB):
@@ -86,33 +91,51 @@ def tile_rnn_model_b_kernel(tc, x, right, wl, bl, wp, bp, offs, out):
                 nc.scalar.activation(h[:, m, :], bank[:], RELU, bias=twice_bl[:, m : m + 1])
             return h
 
-        def project(h, level, c):
+        def project(h, first):
             bank = label_banks.tile([P, C], F32, name="label_bank")
             for k in range(KB):
                 nc.tensor.matmul(
                     bank[:], wp_sb[:, k, :], h[:, k, :], start=(k == 0), stop=(k == KB - 1)
                 )
             labels = staged.tile([P, C], F32, name="labels")
-            nc.vector.tensor_scalar_add(labels[:], bank[:], bp_sb[:, 0:1])
-            first = OUT_START[level] + c * C
+            nc.scalar.activation(labels[:], bank[:], IDENTITY, bias=bp_sb[:, 0:1])
             nc.sync.dma_start(out[:, first : first + C], labels[:])
 
-        def subtree(level, c):
-            if level == 1:
-                s = leaf_sums(c)
-            else:
-                s = nodes.tile([P, KB, C], BF16, name=f"s{level - 1}")
-                for side in range(2):
-                    child = subtree(level - 1, 2 * c + side)
-                    for k in range(KB):
-                        nc.vector.tensor_tensor(
-                            s[:, k, side * HALF : (side + 1) * HALF],
-                            child[:, k, 0:C:2],
-                            child[:, k, 1:C:2],
-                            ADD,
-                        )
-            h = layer(s, level)
-            project(h, level, c)
-            return h
+        leaf_inputs = {c: leaf_sums(c) for c in range(AHEAD)}
+        inputs_of = {}
+        complete = []
+        made = []
 
-        subtree(LEVELS, 0)
+        def chunk(level, c):
+            h = layer(leaf_inputs[c] if level == 1 else inputs_of[(level, c)])
+            if level == 1 and c + AHEAD < N // C:
+                leaf_inputs[c + AHEAD] = leaf_sums(c + AHEAD)
+            if level < LEVELS:
+                parent = (level + 1, c // 2)
+                if parent not in inputs_of:
+                    inputs_of[parent] = inputs.tile([P, KB, C], BF16, name=f"s{level}")
+                side = c % 2
+                for k in range(KB):
+                    nc.vector.tensor_tensor(
+                        inputs_of[parent][:, k, side * HALF : (side + 1) * HALF],
+                        h[:, k, 0:C:2],
+                        h[:, k, 1:C:2],
+                        ADD,
+                    )
+                if side == 1:
+                    complete.append(parent)
+            if made:
+                project(*made[-1])
+            made.append((h, OUT_START[level] + c * C))
+
+        taken = 0
+        for c in range(N // C):
+            one_waits = taken < len(complete)
+            chunk(1, c)
+            if one_waits:
+                chunk(*complete[taken])
+                taken += 1
+        while taken < len(complete):
+            chunk(*complete[taken])
+            taken += 1
+        project(*made[-1])

@@ -29,7 +29,7 @@ def tile_rnn_model_b_kernel(tc, x, right, wl, bl, wp, bp, offs, out):
         tc.tile_pool(name="held", bufs=1) as held,
         tc.tile_pool(name="leaves", bufs=N // C) as leaves,
         tc.tile_pool(name="sums", bufs=4) as sums,
-        tc.tile_pool(name="inputs", bufs=AHEAD + 2) as inputs,
+        tc.tile_pool(name="inputs", bufs=AHEAD + 1) as inputs,
         tc.tile_pool(name="hidden", bufs=4) as hidden,
         tc.tile_pool(name="staged", bufs=3) as staged,
         tc.psum_pool(name="layer_banks", bufs=5) as layer_banks,

@@ -18,22 +18,49 @@ C = 512
 HALF = C // 2
 OUT_START = {t: sum(N >> (u - 1) for u in range(1, t)) for t in range(1, LEVELS + 1)}
 OUT_COLUMNS = OUT_START[LEVELS] + (N >> (LEVELS - 1))
-AHEAD = 2
+PSUM_BANKS = 8
 
 FLOPS = 2 * D * (D + LABELS) * OUT_COLUMNS
+
+LOOK_AHEAD = 5
+ROUND_AHEAD = 2
+INPUT_BLOCKS = 3
+PAIRS_AHEAD = 2
+PROJECT_BEHIND = 3
+PROJECT_BEAT = 2
+LAST_PIECES = 2
+
+
+def chunk_order():
+    order = []
+    place_of = {}
+    for level in range(1, LEVELS + 1):
+        for c in range((N >> (level - 1)) // C):
+            if level > 1:
+                while len(order) < place_of[(level - 1, 2 * c + 1)] + 2:
+                    order.append(None)
+            place_of[(level, c)] = len(order)
+            order.append((level, c))
+    return order
 
 
 def tile_rnn_model_b_kernel(tc, x, right, wl, bl, wp, bp, offs, out):
     nc = tc.nc
+    order = chunk_order()
+    block_of_beat = {
+        KB * place + k: (chunk, k)
+        for place, chunk in enumerate(order)
+        if chunk is not None
+        for k in range(KB)
+    }
     with (
         tc.tile_pool(name="held", bufs=1) as held,
         tc.tile_pool(name="leaves", bufs=N // C) as leaves,
-        tc.tile_pool(name="sums", bufs=4) as sums,
-        tc.tile_pool(name="inputs", bufs=AHEAD + 1) as inputs,
-        tc.tile_pool(name="hidden", bufs=4) as hidden,
+        tc.tile_pool(name="sums", bufs=LOOK_AHEAD - ROUND_AHEAD + 1) as sums,
+        tc.tile_pool(name="blocks", bufs=INPUT_BLOCKS) as blocks,
+        tc.tile_pool(name="hidden", bufs=N // C + 2) as hidden,
         tc.tile_pool(name="staged", bufs=3) as staged,
-        tc.psum_pool(name="layer_banks", bufs=5) as layer_banks,
-        tc.psum_pool(name="label_banks", bufs=3) as label_banks,
+        tc.psum_pool(name="banks", bufs=PSUM_BANKS) as banks,
     ):
         offsets = held.tile([P, N // 16], U16, name="offsets")
         nc.sync.dma_start(offsets[:], offs)
@@ -63,79 +90,110 @@ def tile_rnn_model_b_kernel(tc, x, right, wl, bl, wp, bp, offs, out):
         bp_sb = held.tile([P, 1], F32, name="bp_sb")
         nc.scalar.dma_start(bp_sb[:], bp)
         twice_bl = held.tile([P, KB], F32, name="twice_bl")
-        nc.vector.tensor_scalar_mul(twice_bl[:], bl_sb[:], 2.0)
+        nc.scalar.mul(twice_bl[:], bl_sb[:], 2.0)
 
-        def leaf_sums(c):
-            s = inputs.tile([P, KB, C], BF16, name="s0")
+        exact_of = {}
+        block_of = {}
+        banks_of = {}
+        h_of = {}
+        labels_banks_of = {}
+
+        def look_up(c, k):
+            exact = sums.tile([P, C], F32, name="exact")
             piece = offsets[:, c * (C // 16) : (c + 1) * (C // 16)]
-            for k in range(KB):
-                exact = sums.tile([P, C], F32, name="exact")
-                nc.vector.tensor_tensor(
-                    exact[:], table[k][:].indirect(piece), right_chunks[c][:, k, :], ADD
-                )
-                nc.scalar.copy(s[:, k, :], exact[:])
-            return s
+            nc.vector.tensor_tensor(
+                exact[:], table[k][:].indirect(piece), right_chunks[c][:, k, :], ADD
+            )
+            exact_of[(c, k)] = exact
 
-        def layer(s):
-            h = hidden.tile([P, KB, C], BF16, name="h")
+        def round_leaves(c, k):
+            block = blocks.tile([P, C], BF16, name="block")
+            nc.scalar.copy(block[:], exact_of[(c, k)][:])
+            block_of[((1, c), k)] = block
+
+        def multiply(chunk, k):
+            if k == 0:
+                banks_of[chunk] = [banks.tile([P, C], F32, name="bank") for m in range(KB)]
             for m in range(KB):
-                bank = layer_banks.tile([P, C], F32, name="bank")
+                nc.tensor.matmul(
+                    banks_of[chunk][m][:],
+                    wl_sb[:, k, m * P : (m + 1) * P],
+                    block_of[(chunk, k)][:],
+                    start=(k == 0),
+                    stop=(k == KB - 1),
+                )
+
+        def relu(chunk, m):
+            if m == 0:
+                h_of[chunk] = hidden.tile([P, KB, C], BF16, name="h")
+            nc.scalar.activation(
+                h_of[chunk][:, m, :], banks_of[chunk][m][:], RELU, bias=twice_bl[:, m : m + 1]
+            )
+
+        def sum_pairs(chunk, k):
+            level, c = chunk
+            block = blocks.tile([P, C], BF16, name="block")
+            block_of[(chunk, k)] = block
+            for side in range(2):
+                h = h_of[(level - 1, 2 * c + side)]
+                nc.vector.tensor_tensor(
+                    block[:, side * HALF : (side + 1) * HALF],
+                    h[:, k, 0:C:2],
+                    h[:, k, 1:C:2],
+                    ADD,
+                )
+
+        def pieces_of(chunk):
+            pieces = LAST_PIECES if chunk == order[-1] else 1
+            return [(a, C // pieces) for a in range(0, C, C // pieces)]
+
+        def project(chunk):
+            labels_banks_of[chunk] = []
+            for a, w in pieces_of(chunk):
+                bank = banks.tile([P, w], F32, name="bank")
                 for k in range(KB):
                     nc.tensor.matmul(
                         bank[:],
-                        wl_sb[:, k, m * P : (m + 1) * P],
-                        s[:, k, :],
+                        wp_sb[:, k, :],
+                        h_of[chunk][:, k, a : a + w],
                         start=(k == 0),
                         stop=(k == KB - 1),
                     )
-                nc.scalar.activation(h[:, m, :], bank[:], RELU, bias=twice_bl[:, m : m + 1])
-            return h
+                labels_banks_of[chunk].append(bank)
 
-        def project(h, first):
-            bank = label_banks.tile([P, C], F32, name="label_bank")
-            for k in range(KB):
-                nc.tensor.matmul(
-                    bank[:], wp_sb[:, k, :], h[:, k, :], start=(k == 0), stop=(k == KB - 1)
-                )
-            labels = staged.tile([P, C], F32, name="labels")
-            nc.scalar.activation(labels[:], bank[:], IDENTITY, bias=bp_sb[:, 0:1])
-            nc.sync.dma_start(out[:, first : first + C], labels[:])
+        def store_labels(chunk):
+            first = OUT_START[chunk[0]] + chunk[1] * C
+            for bank, (a, w) in zip(labels_banks_of[chunk], pieces_of(chunk)):
+                labels = staged.tile([P, w], F32, name="labels")
+                nc.scalar.activation(labels[:], bank[:], IDENTITY, bias=bp_sb[:, 0:1])
+                nc.sync.dma_start(out[:, first + a : first + a + w], labels[:])
 
-        leaf_inputs = {c: leaf_sums(c) for c in range(AHEAD)}
-        inputs_of = {}
-        complete = []
-        made = []
+        def chunk_at(place):
+            return order[place] if 0 <= place < len(order) else None
 
-        def chunk(level, c):
-            h = layer(leaf_inputs[c] if level == 1 else inputs_of[(level, c)])
-            if level == 1 and c + AHEAD < N // C:
-                leaf_inputs[c + AHEAD] = leaf_sums(c + AHEAD)
-            if level < LEVELS:
-                parent = (level + 1, c // 2)
-                if parent not in inputs_of:
-                    inputs_of[parent] = inputs.tile([P, KB, C], BF16, name=f"s{level}")
-                side = c % 2
-                for k in range(KB):
-                    nc.vector.tensor_tensor(
-                        inputs_of[parent][:, k, side * HALF : (side + 1) * HALF],
-                        h[:, k, 0:C:2],
-                        h[:, k, 1:C:2],
-                        ADD,
-                    )
-                if side == 1:
-                    complete.append(parent)
-            if made:
-                project(*made[-1])
-            made.append((h, OUT_START[level] + c * C))
+        def block_ahead(beat, ahead, leaves_wanted):
+            chunk, k = block_of_beat.get(beat + ahead, (None, 0))
+            if chunk is not None and (chunk[0] == 1) == leaves_wanted:
+                return chunk, k
+            return None, 0
 
-        taken = 0
-        for c in range(N // C):
-            one_waits = taken < len(complete)
-            chunk(1, c)
-            if one_waits:
-                chunk(*complete[taken])
-                taken += 1
-        while taken < len(complete):
-            chunk(*complete[taken])
-            taken += 1
-        project(*made[-1])
+        for beat in range(-LOOK_AHEAD, KB * (len(order) + PROJECT_BEHIND + 1)):
+            place, k = divmod(beat, KB)
+            to_project = chunk_at(place - PROJECT_BEHIND)
+            if chunk_at(place - 1) is not None:
+                relu(chunk_at(place - 1), k)
+            chunk, block = block_ahead(beat, ROUND_AHEAD, True)
+            if chunk is not None:
+                round_leaves(chunk[1], block)
+            if k == PROJECT_BEAT + 1 and to_project is not None:
+                store_labels(to_project)
+            chunk, block = block_ahead(beat, PAIRS_AHEAD, False)
+            if chunk is not None:
+                sum_pairs(chunk, block)
+            chunk, block = block_ahead(beat, LOOK_AHEAD, True)
+            if chunk is not None:
+                look_up(chunk[1], block)
+            if chunk_at(place) is not None:
+                multiply(chunk_at(place), k)
+            if k == PROJECT_BEAT and to_project is not None:
+                project(to_project)

@@ -27,7 +27,7 @@ ROUND_AHEAD = 2
 INPUT_BLOCKS = 3
 PAIRS_AHEAD = 2
 PROJECT_BEHIND = 3
-PROJECT_BEAT = 2
+PROJECT_BEAT = 1
 LAST_PIECES = 2
 
 
@@ -79,9 +79,11 @@ def tile_rnn_model_b_kernel(tc, x, right, wl, bl, wp, bp, offs, out):
                 if c == 0:
                     nc.sync.dma_start(table[k][:], x_blocks[k])
                 nc.sync.dma_start(right_c[:, k, :], right_blocks[k][:, c * C : (c + 1) * C])
-                if c == 0:
-                    nc.sync.dma_start(wl_sb[:, k, :], wl_blocks[k])
+                if c == 0 and k > 0:
+                    nc.sync.dma_start(wl_sb[:, k - 1, :], wl_blocks[k - 1])
             if c == 0:
+                nc.sync.dma_start(wl_sb[:, KB - 1, :], wl_blocks[KB - 1])
+            if c == PROJECT_BEHIND - 1:
                 nc.sync.dma_start(wp_sb[:], wp.rearrange("(k p) l -> p k l", p=P))
             right_chunks.append(right_c)
 

@@ -4,6 +4,7 @@ F32 = mybir.dt.float32
 BF16 = mybir.dt.bfloat16
 U16 = mybir.dt.uint16
 ADD = mybir.AluOpType.add
+MAX = mybir.AluOpType.max
 RELU = mybir.ActivationFunctionType.Relu
 IDENTITY = mybir.ActivationFunctionType.Identity
 
@@ -28,6 +29,7 @@ INPUT_BLOCKS = 3
 PAIRS_AHEAD = 2
 PROJECT_BEHIND = 3
 PROJECT_BEAT = 1
+WL_BEHIND = 2
 LAST_PIECES = 2
 
 
@@ -68,6 +70,8 @@ def tile_rnn_model_b_kernel(tc, x, right, wl, bl, wp, bp, offs, out):
         table = [held.tile([P, WORDS], F32, name=f"table{k}") for k in range(KB)]
         wl_sb = held.tile([P, KB, D], BF16, name="wl_sb")
         wp_sb = held.tile([P, KB, LABELS], BF16, name="wp_sb")
+        bl_sb = held.tile([P, KB], F32, name="bl_sb")
+        bp_sb = held.tile([P, 1], F32, name="bp_sb")
         x_blocks = x.rearrange("(k p) s -> k p s", p=P)
         right_blocks = right.rearrange("(k p) n -> k p n", p=P)
         wl_blocks = wl.rearrange("(k p) m -> k p m", p=P)
@@ -79,20 +83,19 @@ def tile_rnn_model_b_kernel(tc, x, right, wl, bl, wp, bp, offs, out):
                 if c == 0:
                     nc.sync.dma_start(table[k][:], x_blocks[k])
                 nc.sync.dma_start(right_c[:, k, :], right_blocks[k][:, c * C : (c + 1) * C])
-                if c == 0 and k > 0:
-                    nc.sync.dma_start(wl_sb[:, k - 1, :], wl_blocks[k - 1])
+                if c == 0 and k >= WL_BEHIND:
+                    nc.sync.dma_start(wl_sb[:, k - WL_BEHIND, :], wl_blocks[k - WL_BEHIND])
             if c == 0:
-                nc.sync.dma_start(wl_sb[:, KB - 1, :], wl_blocks[KB - 1])
+                for k in range(KB - WL_BEHIND, KB):
+                    nc.sync.dma_start(wl_sb[:, k, :], wl_blocks[k])
+                nc.sync.dma_start(bl_sb[:], bl.rearrange("(a p) o -> p (a o)", p=P))
             if c == PROJECT_BEHIND - 1:
                 nc.sync.dma_start(wp_sb[:], wp.rearrange("(k p) l -> p k l", p=P))
+                nc.sync.dma_start(bp_sb[:], bp)
             right_chunks.append(right_c)
 
-        bl_sb = held.tile([P, KB], F32, name="bl_sb")
-        nc.scalar.dma_start(bl_sb[:], bl.rearrange("(a p) o -> p (a o)", p=P))
-        bp_sb = held.tile([P, 1], F32, name="bp_sb")
-        nc.scalar.dma_start(bp_sb[:], bp)
         twice_bl = held.tile([P, KB], F32, name="twice_bl")
-        nc.scalar.mul(twice_bl[:], bl_sb[:], 2.0)
+        nc.gpsimd.tensor_scalar_mul(twice_bl[:], bl_sb[:], 2.0)
 
         exact_of = {}
         block_of = {}
@@ -128,9 +131,14 @@ def tile_rnn_model_b_kernel(tc, x, right, wl, bl, wp, bp, offs, out):
         def relu(chunk, m):
             if m == 0:
                 h_of[chunk] = hidden.tile([P, KB, C], BF16, name="h")
-            nc.scalar.activation(
-                h_of[chunk][:, m, :], banks_of[chunk][m][:], RELU, bias=twice_bl[:, m : m + 1]
-            )
+            if chunk == order[-1] and m % 2 == 1:
+                nc.vector.tensor_scalar(
+                    h_of[chunk][:, m, :], banks_of[chunk][m][:], twice_bl[:, m : m + 1], 0.0, ADD, MAX
+                )
+            else:
+                nc.scalar.activation(
+                    h_of[chunk][:, m, :], banks_of[chunk][m][:], RELU, bias=twice_bl[:, m : m + 1]
+                )
 
         def sum_pairs(chunk, k):
             level, c = chunk
@@ -167,7 +175,10 @@ def tile_rnn_model_b_kernel(tc, x, right, wl, bl, wp, bp, offs, out):
             first = OUT_START[chunk[0]] + chunk[1] * C
             for bank, (a, w) in zip(labels_banks_of[chunk], pieces_of(chunk)):
                 labels = staged.tile([P, w], F32, name="labels")
-                nc.scalar.activation(labels[:], bank[:], IDENTITY, bias=bp_sb[:, 0:1])
+                if chunk == order[-1] and a == 0:
+                    nc.vector.tensor_scalar_add(labels[:], bank[:], bp_sb[:, 0:1])
+                else:
+                    nc.scalar.activation(labels[:], bank[:], IDENTITY, bias=bp_sb[:, 0:1])
                 nc.sync.dma_start(out[:, first + a : first + a + w], labels[:])
 
         def chunk_at(place):

@@ -83,12 +83,13 @@ def tile_rnn_model_b_kernel(tc, x, right, wl, bl, wp, bp, offs, out):
                 if c == 0:
                     nc.sync.dma_start(table[k][:], x_blocks[k])
                 nc.sync.dma_start(right_c[:, k, :], right_blocks[k][:, c * C : (c + 1) * C])
+                if c == 0 and k == 1:
+                    nc.sync.dma_start(bl_sb[:], bl.rearrange("(a p) o -> p (a o)", p=P))
                 if c == 0 and k >= WL_BEHIND:
                     nc.sync.dma_start(wl_sb[:, k - WL_BEHIND, :], wl_blocks[k - WL_BEHIND])
             if c == 0:
                 for k in range(KB - WL_BEHIND, KB):
                     nc.sync.dma_start(wl_sb[:, k, :], wl_blocks[k])
-                nc.sync.dma_start(bl_sb[:], bl.rearrange("(a p) o -> p (a o)", p=P))
             if c == PROJECT_BEHIND - 1:
                 nc.sync.dma_start(wp_sb[:], wp.rearrange("(k p) l -> p k l", p=P))
                 nc.sync.dma_start(bp_sb[:], bp)

@@ -29,6 +29,7 @@ INPUT_BLOCKS = 3
 PAIRS_AHEAD = 2
 PROJECT_BEHIND = 3
 PROJECT_BEAT = 1
+FINE_CHUNKS = 2
 WL_BEHIND = 2
 LAST_PIECES = 2
 
@@ -57,7 +58,7 @@ def tile_rnn_model_b_kernel(tc, x, right, wl, bl, wp, bp, offs, out):
     }
     with (
         tc.tile_pool(name="held", bufs=1) as held,
-        tc.tile_pool(name="leaves", bufs=N // C) as leaves,
+        tc.tile_pool(name="leaves", bufs=(N // C - FINE_CHUNKS) // 2) as leaves,
         tc.tile_pool(name="sums", bufs=LOOK_AHEAD - ROUND_AHEAD + 1) as sums,
         tc.tile_pool(name="blocks", bufs=INPUT_BLOCKS) as blocks,
         tc.tile_pool(name="hidden", bufs=N // C + 2) as hidden,
@@ -76,9 +77,10 @@ def tile_rnn_model_b_kernel(tc, x, right, wl, bl, wp, bp, offs, out):
         right_blocks = right.rearrange("(k p) n -> k p n", p=P)
         wl_blocks = wl.rearrange("(k p) m -> k p m", p=P)
 
-        right_chunks = []
-        for c in range(N // C):
+        right_of = {}
+        for c in range(0, FINE_CHUNKS):
             right_c = leaves.tile([P, KB, C], F32, name="right_c")
+            right_of[c] = (right_c, 0)
             for k in range(KB):
                 if c == 0:
                     nc.sync.dma_start(table[k][:], x_blocks[k])
@@ -90,10 +92,15 @@ def tile_rnn_model_b_kernel(tc, x, right, wl, bl, wp, bp, offs, out):
             if c == 0:
                 for k in range(KB - WL_BEHIND, KB):
                     nc.sync.dma_start(wl_sb[:, k, :], wl_blocks[k])
-            if c == PROJECT_BEHIND - 1:
+        for c in range(FINE_CHUNKS, N // C, 2):
+            right_pair = leaves.tile([P, KB, 2 * C], F32, name="right_pair")
+            right_of[c] = (right_pair, 0)
+            right_of[c + 1] = (right_pair, C)
+            for k in range(KB):
+                nc.sync.dma_start(right_pair[:, k, :], right_blocks[k][:, c * C : (c + 2) * C])
+            if c == FINE_CHUNKS:
                 nc.sync.dma_start(wp_sb[:], wp.rearrange("(k p) l -> p k l", p=P))
                 nc.sync.dma_start(bp_sb[:], bp)
-            right_chunks.append(right_c)
 
         twice_bl = held.tile([P, KB], F32, name="twice_bl")
         nc.gpsimd.tensor_scalar_mul(twice_bl[:], bl_sb[:], 2.0)
@@ -107,8 +114,9 @@ def tile_rnn_model_b_kernel(tc, x, right, wl, bl, wp, bp, offs, out):
         def look_up(c, k):
             exact = sums.tile([P, C], F32, name="exact")
             piece = offsets[:, c * (C // 16) : (c + 1) * (C // 16)]
+            right_tile, first = right_of[c]
             nc.vector.tensor_tensor(
-                exact[:], table[k][:].indirect(piece), right_chunks[c][:, k, :], ADD
+                exact[:], table[k][:].indirect(piece), right_tile[:, k, first : first + C], ADD
             )
             exact_of[(c, k)] = exact
 

@@ -87,11 +87,9 @@ def tile_rnn_model_b_kernel(tc, x, right, wl, bl, wp, bp, offs, out):
                 nc.sync.dma_start(right_c[:, k, :], right_blocks[k][:, c * C : (c + 1) * C])
                 if c == 0 and k == 1:
                     nc.sync.dma_start(bl_sb[:], bl.rearrange("(a p) o -> p (a o)", p=P))
-                if c == 0 and k >= WL_BEHIND:
-                    nc.sync.dma_start(wl_sb[:, k - WL_BEHIND, :], wl_blocks[k - WL_BEHIND])
-            if c == 0:
-                for k in range(KB - WL_BEHIND, KB):
-                    nc.sync.dma_start(wl_sb[:, k, :], wl_blocks[k])
+                wl_block = c * KB + k - WL_BEHIND
+                if 0 <= wl_block < KB:
+                    nc.sync.dma_start(wl_sb[:, wl_block, :], wl_blocks[wl_block])
         for c in range(FINE_CHUNKS, N // C, 2):
             right_pair = leaves.tile([P, KB, 2 * C], F32, name="right_pair")
             right_of[c] = (right_pair, 0)

@@ -30,20 +30,28 @@ PAIRS_AHEAD = 2
 PROJECT_BEHIND = 3
 PROJECT_BEAT = 1
 FINE_CHUNKS = 2
+STAGED = 4
 WL_BEHIND = 2
-LAST_PIECES = 2
+
+
+def width(level):
+    return C if level < LEVELS else HALF
+
+
+def children(chunk):
+    level, c = chunk
+    per_chunk = width(level) // HALF
+    return [(level - 1, per_chunk * c + side) for side in range(per_chunk)]
 
 
 def chunk_order():
-    order = []
-    place_of = {}
-    for level in range(1, LEVELS + 1):
-        for c in range((N >> (level - 1)) // C):
-            if level > 1:
-                while len(order) < place_of[(level - 1, 2 * c + 1)] + 2:
-                    order.append(None)
-            place_of[(level, c)] = len(order)
-            order.append((level, c))
+    order = [
+        (level, c)
+        for level in range(1, LEVELS + 1)
+        for c in range((N >> (level - 1)) // width(level))
+    ]
+    for place, chunk in enumerate(order):
+        assert chunk[0] == 1 or order.index(children(chunk)[-1]) + 2 <= place
     return order
 
 
@@ -53,7 +61,6 @@ def tile_rnn_model_b_kernel(tc, x, right, wl, bl, wp, bp, offs, out):
     block_of_beat = {
         KB * place + k: (chunk, k)
         for place, chunk in enumerate(order)
-        if chunk is not None
         for k in range(KB)
     }
     with (
@@ -62,7 +69,7 @@ def tile_rnn_model_b_kernel(tc, x, right, wl, bl, wp, bp, offs, out):
         tc.tile_pool(name="sums", bufs=LOOK_AHEAD - ROUND_AHEAD + 1) as sums,
         tc.tile_pool(name="blocks", bufs=INPUT_BLOCKS) as blocks,
         tc.tile_pool(name="hidden", bufs=N // C + 2) as hidden,
-        tc.tile_pool(name="staged", bufs=3) as staged,
+        tc.tile_pool(name="staged", bufs=STAGED) as staged,
         tc.psum_pool(name="banks", bufs=PSUM_BANKS) as banks,
     ):
         offsets = held.tile([P, N // 16], U16, name="offsets")
@@ -107,7 +114,7 @@ def tile_rnn_model_b_kernel(tc, x, right, wl, bl, wp, bp, offs, out):
         block_of = {}
         banks_of = {}
         h_of = {}
-        labels_banks_of = {}
+        labels_bank_of = {}
 
         def look_up(c, k):
             exact = sums.tile([P, C], F32, name="exact")
@@ -125,7 +132,9 @@ def tile_rnn_model_b_kernel(tc, x, right, wl, bl, wp, bp, offs, out):
 
         def multiply(chunk, k):
             if k == 0:
-                banks_of[chunk] = [banks.tile([P, C], F32, name="bank") for m in range(KB)]
+                banks_of[chunk] = [
+                    banks.tile([P, width(chunk[0])], F32, name="bank") for m in range(KB)
+                ]
             for m in range(KB):
                 nc.tensor.matmul(
                     banks_of[chunk][m][:],
@@ -137,7 +146,7 @@ def tile_rnn_model_b_kernel(tc, x, right, wl, bl, wp, bp, offs, out):
 
         def relu(chunk, m):
             if m == 0:
-                h_of[chunk] = hidden.tile([P, KB, C], BF16, name="h")
+                h_of[chunk] = hidden.tile([P, KB, width(chunk[0])], BF16, name="h")
             if chunk == order[-1] and m % 2 == 1:
                 nc.vector.tensor_scalar(
                     h_of[chunk][:, m, :], banks_of[chunk][m][:], twice_bl[:, m : m + 1], 0.0, ADD, MAX
@@ -148,11 +157,10 @@ def tile_rnn_model_b_kernel(tc, x, right, wl, bl, wp, bp, offs, out):
                 )
 
         def sum_pairs(chunk, k):
-            level, c = chunk
-            block = blocks.tile([P, C], BF16, name="block")
+            block = blocks.tile([P, width(chunk[0])], BF16, name="block")
             block_of[(chunk, k)] = block
-            for side in range(2):
-                h = h_of[(level - 1, 2 * c + side)]
+            for side, child in enumerate(children(chunk)):
+                h = h_of[child]
                 nc.vector.tensor_tensor(
                     block[:, side * HALF : (side + 1) * HALF],
                     h[:, k, 0:C:2],
@@ -160,33 +168,26 @@ def tile_rnn_model_b_kernel(tc, x, right, wl, bl, wp, bp, offs, out):
                     ADD,
                 )
 
-        def pieces_of(chunk):
-            pieces = LAST_PIECES if chunk == order[-1] else 1
-            return [(a, C // pieces) for a in range(0, C, C // pieces)]
-
         def project(chunk):
-            labels_banks_of[chunk] = []
-            for a, w in pieces_of(chunk):
-                bank = banks.tile([P, w], F32, name="bank")
-                for k in range(KB):
-                    nc.tensor.matmul(
-                        bank[:],
-                        wp_sb[:, k, :],
-                        h_of[chunk][:, k, a : a + w],
-                        start=(k == 0),
-                        stop=(k == KB - 1),
-                    )
-                labels_banks_of[chunk].append(bank)
+            bank = banks.tile([P, width(chunk[0])], F32, name="bank")
+            for k in range(KB):
+                nc.tensor.matmul(
+                    bank[:], wp_sb[:, k, :], h_of[chunk][:, k, :], start=(k == 0), stop=(k == KB - 1)
+                )
+            labels_bank_of[chunk] = bank
 
         def store_labels(chunk):
-            first = OUT_START[chunk[0]] + chunk[1] * C
-            for bank, (a, w) in zip(labels_banks_of[chunk], pieces_of(chunk)):
-                labels = staged.tile([P, w], F32, name="labels")
-                if chunk == order[-1] and a == 0:
-                    nc.vector.tensor_scalar_add(labels[:], bank[:], bp_sb[:, 0:1])
-                else:
-                    nc.scalar.activation(labels[:], bank[:], IDENTITY, bias=bp_sb[:, 0:1])
-                nc.sync.dma_start(out[:, first + a : first + a + w], labels[:])
+            level, c = chunk
+            w = width(level)
+            labels = staged.tile([P, w], F32, name="labels")
+            if chunk == order[-2]:
+                nc.vector.tensor_scalar_add(labels[:], labels_bank_of[chunk][:], bp_sb[:, 0:1])
+            else:
+                nc.scalar.activation(
+                    labels[:], labels_bank_of[chunk][:], IDENTITY, bias=bp_sb[:, 0:1]
+                )
+            first = OUT_START[level] + c * w
+            nc.sync.dma_start(out[:, first : first + w], labels[:])
 
         def chunk_at(place):
             return order[place] if 0 <= place < len(order) else None

import concourse.mybir as mybir

F32 = mybir.dt.float32
BF16 = mybir.dt.bfloat16
U16 = mybir.dt.uint16
ADD = mybir.AluOpType.add
MAX = mybir.AluOpType.max
RELU = mybir.ActivationFunctionType.Relu
IDENTITY = mybir.ActivationFunctionType.Identity

P = 128
D = 512
KB = D // P
WORDS = 512
N = 4096
LABELS = 128
LEVELS = 4
C = 512
HALF = C // 2
OUT_START = {t: sum(N >> (u - 1) for u in range(1, t)) for t in range(1, LEVELS + 1)}
OUT_COLUMNS = OUT_START[LEVELS] + (N >> (LEVELS - 1))
PSUM_BANKS = 8

FLOPS = 2 * D * (D + LABELS) * OUT_COLUMNS

LOOK_AHEAD = 5
ROUND_AHEAD = 2
INPUT_BLOCKS = 3
PAIRS_AHEAD = 2
PROJECT_BEHIND = 3
PROJECT_BEAT = 1
FINE_CHUNKS = 2
STAGED = 4
WL_BEHIND = 2


def width(level):
    return C if level < LEVELS else HALF


def children(chunk):
    level, c = chunk
    per_chunk = width(level) // HALF
    return [(level - 1, per_chunk * c + side) for side in range(per_chunk)]


def chunk_order():
    order = [
        (level, c)
        for level in range(1, LEVELS + 1)
        for c in range((N >> (level - 1)) // width(level))
    ]
    for place, chunk in enumerate(order):
        assert chunk[0] == 1 or order.index(children(chunk)[-1]) + 2 <= place
    return order


def tile_rnn_model_b_kernel(tc, x, right, wl, bl, wp, bp, offs, out):
    nc = tc.nc
    order = chunk_order()
    block_of_beat = {
        KB * place + k: (chunk, k)
        for place, chunk in enumerate(order)
        for k in range(KB)
    }
    with (
        tc.tile_pool(name="held", bufs=1) as held,
        tc.tile_pool(name="leaves", bufs=(N // C - FINE_CHUNKS) // 2) as leaves,
        tc.tile_pool(name="sums", bufs=LOOK_AHEAD - ROUND_AHEAD + 1) as sums,
        tc.tile_pool(name="blocks", bufs=INPUT_BLOCKS) as blocks,
        tc.tile_pool(name="hidden", bufs=N // C + 2) as hidden,
        tc.tile_pool(name="staged", bufs=STAGED) as staged,
        tc.psum_pool(name="banks", bufs=PSUM_BANKS) as banks,
    ):
        offsets = held.tile([P, N // 16], U16, name="offsets")
        nc.sync.dma_start(offsets[:], offs)

        table = [held.tile([P, WORDS], F32, name=f"table{k}") for k in range(KB)]
        wl_sb = held.tile([P, KB, D], BF16, name="wl_sb")
        wp_sb = held.tile([P, KB, LABELS], BF16, name="wp_sb")
        bl_sb = held.tile([P, KB], F32, name="bl_sb")
        bp_sb = held.tile([P, 1], F32, name="bp_sb")
        x_blocks = x.rearrange("(k p) s -> k p s", p=P)
        right_blocks = right.rearrange("(k p) n -> k p n", p=P)
        wl_blocks = wl.rearrange("(k p) m -> k p m", p=P)

        right_of = {}
        for c in range(0, FINE_CHUNKS):
            right_c = leaves.tile([P, KB, C], F32, name="right_c")
            right_of[c] = (right_c, 0)
            for k in range(KB):
                if c == 0:
                    nc.sync.dma_start(table[k][:], x_blocks[k])
                nc.sync.dma_start(right_c[:, k, :], right_blocks[k][:, c * C : (c + 1) * C])
                if c == 0 and k == 1:
                    nc.sync.dma_start(bl_sb[:], bl.rearrange("(a p) o -> p (a o)", p=P))
                wl_block = c * KB + k - WL_BEHIND
                if 0 <= wl_block < KB:
                    nc.sync.dma_start(wl_sb[:, wl_block, :], wl_blocks[wl_block])
        for c in range(FINE_CHUNKS, N // C, 2):
            right_pair = leaves.tile([P, KB, 2 * C], F32, name="right_pair")
            right_of[c] = (right_pair, 0)
            right_of[c + 1] = (right_pair, C)
            for k in range(KB):
                nc.sync.dma_start(right_pair[:, k, :], right_blocks[k][:, c * C : (c + 2) * C])
            if c == FINE_CHUNKS:
                nc.sync.dma_start(wp_sb[:], wp.rearrange("(k p) l -> p k l", p=P))
                nc.sync.dma_start(bp_sb[:], bp)

        twice_bl = held.tile([P, KB], F32, name="twice_bl")
        nc.gpsimd.tensor_scalar_mul(twice_bl[:], bl_sb[:], 2.0)

        exact_of = {}
        block_of = {}
        banks_of = {}
        h_of = {}
        labels_bank_of = {}

        def look_up(c, k):
            exact = sums.tile([P, C], F32, name="exact")
            piece = offsets[:, c * (C // 16) : (c + 1) * (C // 16)]
            right_tile, first = right_of[c]
            nc.vector.tensor_tensor(
                exact[:], table[k][:].indirect(piece), right_tile[:, k, first : first + C], ADD
            )
            exact_of[(c, k)] = exact

        def round_leaves(c, k):
            block = blocks.tile([P, C], BF16, name="block")
            nc.scalar.copy(block[:], exact_of[(c, k)][:])
            block_of[((1, c), k)] = block

        def multiply(chunk, k):
            if k == 0:
                banks_of[chunk] = [
                    banks.tile([P, width(chunk[0])], F32, name="bank") for m in range(KB)
                ]
            for m in range(KB):
                nc.tensor.matmul(
                    banks_of[chunk][m][:],
                    wl_sb[:, k, m * P : (m + 1) * P],
                    block_of[(chunk, k)][:],
                    start=(k == 0),
                    stop=(k == KB - 1),
                )

        def relu(chunk, m):
            if m == 0:
                h_of[chunk] = hidden.tile([P, KB, width(chunk[0])], BF16, name="h")
            if chunk == order[-1] and m % 2 == 1:
                nc.vector.tensor_scalar(
                    h_of[chunk][:, m, :], banks_of[chunk][m][:], twice_bl[:, m : m + 1], 0.0, ADD, MAX
                )
            else:
                nc.scalar.activation(
                    h_of[chunk][:, m, :], banks_of[chunk][m][:], RELU, bias=twice_bl[:, m : m + 1]
                )

        def sum_pairs(chunk, k):
            block = blocks.tile([P, width(chunk[0])], BF16, name="block")
            block_of[(chunk, k)] = block
            for side, child in enumerate(children(chunk)):
                h = h_of[child]
                nc.vector.tensor_tensor(
                    block[:, side * HALF : (side + 1) * HALF],
                    h[:, k, 0:C:2],
                    h[:, k, 1:C:2],
                    ADD,
                )

        def project(chunk):
            bank = banks.tile([P, width(chunk[0])], F32, name="bank")
            for k in range(KB):
                nc.tensor.matmul(
                    bank[:], wp_sb[:, k, :], h_of[chunk][:, k, :], start=(k == 0), stop=(k == KB - 1)
                )
            labels_bank_of[chunk] = bank

        def store_labels(chunk):
            level, c = chunk
            w = width(level)
            labels = staged.tile([P, w], F32, name="labels")
            if chunk == order[-2]:
                nc.vector.tensor_scalar_add(labels[:], labels_bank_of[chunk][:], bp_sb[:, 0:1])
            else:
                nc.scalar.activation(
                    labels[:], labels_bank_of[chunk][:], IDENTITY, bias=bp_sb[:, 0:1]
                )
            first = OUT_START[level] + c * w
            nc.sync.dma_start(out[:, first : first + w], labels[:])

        def chunk_at(place):
            return order[place] if 0 <= place < len(order) else None

        def block_ahead(beat, ahead, leaves_wanted):
            chunk, k = block_of_beat.get(beat + ahead, (None, 0))
            if chunk is not None and (chunk[0] == 1) == leaves_wanted:
                return chunk, k
            return None, 0

        for beat in range(-LOOK_AHEAD, KB * (len(order) + PROJECT_BEHIND + 1)):
            place, k = divmod(beat, KB)
            to_project = chunk_at(place - PROJECT_BEHIND)
            if chunk_at(place - 1) is not None:
                relu(chunk_at(place - 1), k)
            chunk, block = block_ahead(beat, ROUND_AHEAD, True)
            if chunk is not None:
                round_leaves(chunk[1], block)
            if k == PROJECT_BEAT + 1 and to_project is not None:
                store_labels(to_project)
            chunk, block = block_ahead(beat, PAIRS_AHEAD, False)
            if chunk is not None:
                sum_pairs(chunk, block)
            chunk, block = block_ahead(beat, LOOK_AHEAD, True)
            if chunk is not None:
                look_up(chunk[1], block)
            if chunk_at(place) is not None:
                multiply(chunk_at(place), k)
            if k == PROJECT_BEAT and to_project is not None:
                project(to_project)
